import numpy as np
import ml_dtypes


BF16 = ml_dtypes.bfloat16


def bf(x):
    return np.asarray(x, np.float32).astype(BF16)


def f64(x):
    return np.asarray(x).astype(np.float64)


E2M1 = np.array([0.0, 0.5, 1.0, 1.5, 2.0, 3.0, 4.0, 6.0, -0.0, -0.5, -1.0, -1.5, -2.0, -3.0, -4.0, -6.0])


def pack_weight(w, fmt):
    k, n = w.shape
    w = f64(bf(w)).reshape(k // 32, 32, n)
    amax = np.abs(w).max(1)
    if fmt == "e4m3":
        byte = np.frexp(amax)[1] - 1 + 127 - 7
    else:
        mant, ex = np.frexp(amax / 6.0)
        byte = np.where(mant > 0.5, ex, ex - 1) + 127
    byte = np.clip(np.where(amax > 0, byte, 1), 1, 254)
    scaled = (w * np.exp2(127.0 - byte)[:, None, :]).reshape(k, n).astype(np.float32)
    by_word = np.ascontiguousarray(scaled.reshape(k // 512, 128, 4, n).transpose(0, 1, 3, 2))
    if fmt == "e4m3":
        words = by_word.astype(ml_dtypes.float8_e4m3fn).view(np.uint8)
    else:
        c = by_word.astype(ml_dtypes.float4_e2m1fn).view(np.uint8) & 0xF
        words = c[..., 0::2] | (c[..., 1::2] << 4)
    return np.ascontiguousarray(words), np.ascontiguousarray(byte.astype(np.uint8).reshape(k // 512, 16, n))


def unpack_weight(words, scales, fmt):
    g, p, n, _ = words.shape
    if fmt == "e4m3":
        vals = np.ascontiguousarray(words).view(ml_dtypes.float8_e4m3fn).astype(np.float64)
    else:
        nib = np.empty((g, p, n, 4), np.uint8)
        nib[..., 0::2] = words & 0xF
        nib[..., 1::2] = words >> 4
        vals = E2M1[nib]
    vals = vals * np.repeat(np.exp2(scales.astype(np.float64) - 127.0), 8, axis=1)[..., None]
    return vals.transpose(0, 1, 3, 2).reshape(g * 512, n)

def pack4(w):
    words, scales = pack_weight(w, "e2m1")
    return words.reshape(words.shape[0], 128, -1), scales


def unpack4(words, scales):
    return unpack_weight(words.reshape(words.shape[0], 128, -1, 2), scales, "e2m1")


def kspread(k):
    return np.exp2(np.repeat(np.random.randint(-6, 7, k // 32), 32).astype(np.float64))


B, S, C, H, D = 4, 768, 4096, 8, 256
E = H * D


def rope_tables():
    inv_freq = 1.0 / (10000.0 ** (np.arange(0, D, 2) / D))
    emb = np.repeat(np.outer(np.arange(S), inv_freq), 2, axis=1)
    return np.cos(emb), np.sin(emb)


def rope(t, cos, sin):
    tr = t[..., 0::2]
    ti = t[..., 1::2]
    t_rot = np.stack([-ti, tr], axis=-1).reshape(t.shape)
    return t * cos + t_rot * sin


def setup_inputs():
    s = kspread(C)
    cos, sin = rope_tables()
    x = np.random.standard_normal((B, S, C)) * s
    x_words, x_scales = pack4(np.ascontiguousarray(x.reshape(B * S, C).T))
    Wq = np.random.standard_normal((E, C)) / np.sqrt(C) / s[None, :]
    Wq_words, Wq_scales = pack4(np.ascontiguousarray(Wq.T))
    bq = bf(np.random.standard_normal(E) * 0.1)
    return {"x_words": x_words, "x_scales": x_scales,
            "cos": bf(cos), "sin": bf(sin),
            "Wq_words": Wq_words, "Wq_scales": Wq_scales,
            "bq": bq}


def reference(x_words, x_scales, cos, sin, Wq_words, Wq_scales, bq):
    xq = unpack4(x_words, x_scales).T.reshape(B, S, C)
    y = (xq @ unpack4(Wq_words, Wq_scales)) + f64(bq)
    q = y.reshape(B, S, H, D).transpose(0, 2, 1, 3)
    return np.maximum(rope(q, f64(cos), f64(sin)), 0.0)

@@ -1,0 +1,192 @@
+from contextlib import ExitStack
+
+import concourse.mybir as mybir
+from concourse.masks import make_identity
+
+B, S, C, H, D = 4, 768, 4096, 8, 256
+E = H * D
+FLOPS = 2 * B * S * C * E
+
+F32 = mybir.dt.float32
+BF16 = mybir.dt.bfloat16
+U8 = mybir.dt.uint8
+I32 = mybir.dt.int32
+FP4X4 = mybir.dt.float4_e2m1fn_x4
+ADD = mybir.AluOpType.add
+MULT = mybir.AluOpType.mult
+RELU = mybir.ActivationFunctionType.Relu
+COPY = mybir.ActivationFunctionType.Copy
+
+P = 128
+PASSES = C // 512
+N_TILE = 512
+N_BLOCKS = E // N_TILE
+CHUNK_BLOCKS = 4
+CHUNK_TOKENS = CHUNK_BLOCKS * P
+N_CHUNKS = B * S // CHUNK_TOKENS
+POS_BLOCKS = S // P
+X_BUFS = 2
+
+
+def tile_lineartransformerblock_pa_kernel(tc, x_words, x_scales, cos, sin, Wq_words, Wq_scales, bq, out):
+    nc = tc.nc
+    with ExitStack() as ctx:
+        keep = ctx.enter_context(tc.tile_pool(name="keep", bufs=1))
+        work = ctx.enter_context(tc.tile_pool(name="work", bufs=3))
+        tabs = ctx.enter_context(tc.psum_pool(name="tabs", bufs=1))
+        accs = ctx.enter_context(tc.psum_pool(name="accs", bufs=5))
+        ctx.enter_context(tc.manual_schedule())
+
+        w_codes = []
+        w_planes = []
+        for n in range(N_BLOCKS):
+            w_codes.append(keep.tile([P, PASSES, 2 * N_TILE], U8, name="w_codes%d" % n, align_bytes=64))
+            w_planes.append(keep.tile([P, PASSES, N_TILE], U8, name="w_planes%d" % n, align_bytes=64))
+        x_codes = []
+        x_planes = []
+        for j in range(X_BUFS):
+            x_codes.append(keep.tile([P, PASSES, 2 * CHUNK_TOKENS], U8, name="x_codes%d" % j, align_bytes=64))
+            x_planes.append(keep.tile([P, PASSES, CHUNK_TOKENS], U8, name="x_planes%d" % j, align_bytes=64))
+        brow = keep.tile([P, E], BF16, name="brow")
+        ones = keep.tile([P, P], BF16, name="ones")
+        ident = keep.tile([P, P], BF16, name="ident")
+        tab_sb = keep.tile([P, 2, POS_BLOCKS, D], BF16, name="tab_sb")
+        bias_sb = keep.tile([P, E], F32, name="bias_sb")
+        tab_ps = []
+        for j in range(POS_BLOCKS // 2):
+            tab_ps.append(tabs.tile([P, 4 * D], BF16, name="tab_ps%d" % j))
+
+        def load_codes(dst, src, g0, g1, col0, ncols, dcol0):
+            nc.sync.dma_start(
+                out=dst[:, g0:g1, dcol0 : dcol0 + ncols].bitcast(I32),
+                in_=src[g0:g1, :, col0 : col0 + ncols].rearrange("g p c -> p g c").bitcast(I32),
+            )
+
+        def load_scales(dst, src, g0, g1, col0, ncols):
+            for r in range(4):
+                nc.sync.dma_start(
+                    out=dst[r:P:32, g0:g1, :].bitcast(I32),
+                    in_=src[g0:g1, r:16:4, col0 : col0 + ncols].rearrange("g q n -> q g n").bitcast(I32),
+                )
+
+        def load_x_chunk(c):
+            j = c % X_BUFS
+            load_codes(x_codes[j], x_words, 0, PASSES, 2 * CHUNK_TOKENS * c, 2 * CHUNK_TOKENS, 0)
+            load_scales(x_planes[j], x_scales, 0, PASSES, CHUNK_TOKENS * c, CHUNK_TOKENS)
+
+        def load_w_block(n):
+            load_codes(w_codes[n], Wq_words, 0, PASSES, 2 * N_TILE * n, 2 * N_TILE, 0)
+            load_scales(w_planes[n], Wq_scales, 0, PASSES, N_TILE * n, N_TILE)
+
+        def zero_planes(t):
+            nc.vector.memset(t[:].bitcast(I32), 0)
+
+        nc.vector.memset(brow[:], 0.0)
+        nc.vector.memset(ones[:], 1.0)
+        zero_planes(w_planes[0])
+        zero_planes(x_planes[0])
+        make_identity(nc, ident[:])
+
+        cos_v = cos.rearrange("(k p) d -> p k d", p=P)
+        sin_v = sin.rearrange("(k p) d -> p k d", p=P)
+        nc.scalar.dma_start(out=tab_sb[:, 0, 0:2, :], in_=cos_v[:, 0:2, :])
+        nc.scalar.dma_start(out=tab_sb[:, 1, 0:2, :], in_=sin_v[:, 0:2, :])
+        nc.scalar.dma_start(out=brow[0:1, :], in_=bq.rearrange("(o c) -> o c", o=1))
+
+        half = PASSES // 2
+        load_codes(x_codes[0], x_words, 0, half, 0, 2 * CHUNK_TOKENS, 0)
+        load_codes(w_codes[0], Wq_words, 0, half, 0, 2 * N_TILE, 0)
+        load_scales(w_planes[0], Wq_scales, 0, PASSES, 0, N_TILE)
+        load_scales(x_planes[0], x_scales, 0, PASSES, 0, CHUNK_TOKENS)
+        load_codes(x_codes[0], x_words, half, PASSES, 0, 2 * CHUNK_TOKENS, 0)
+        load_codes(w_codes[0], Wq_words, half, PASSES, 0, 2 * N_TILE, 0)
+
+        nc.scalar.dma_start(out=tab_sb[:, 0, 2:POS_BLOCKS, :], in_=cos_v[:, 2:POS_BLOCKS, :])
+        nc.scalar.dma_start(out=tab_sb[:, 1, 2:POS_BLOCKS, :], in_=sin_v[:, 2:POS_BLOCKS, :])
+
+        for n in range(1, N_BLOCKS):
+            zero_planes(w_planes[n])
+        zero_planes(x_planes[1])
+        load_w_block(1)
+        load_x_chunk(1)
+        load_w_block(2)
+        load_w_block(3)
+
+        def flip_sign(k0, k1):
+            even = tab_sb[:, 1, k0:k1, :].rearrange("p k (i e) -> p k i e", e=2)[:, :, :, 0:1]
+            nc.scalar.activation(out=even, in_=even, func=COPY, scale=-1.0)
+
+        def table_to_psum(j, t):
+            nc.tensor.matmul(
+                tab_ps[j][:, 2 * D * t : 2 * D * (t + 1)],
+                lhsT=ident[:],
+                rhs=tab_sb[:, t, 2 * j : 2 * j + 2, :].rearrange("p k d -> p (k d)"),
+                start=True,
+                stop=True,
+            )
+
+        flip_sign(0, 2)
+        table_to_psum(0, 0)
+        for n in range(N_BLOCKS):
+            pb = accs.tile([P, N_TILE], F32, name="acc")
+            nc.tensor.matmul(pb[:], lhsT=ones[:], rhs=brow[:, N_TILE * n : N_TILE * (n + 1)], start=True, stop=True)
+            nc.scalar.copy(out=bias_sb[:, N_TILE * n : N_TILE * (n + 1)], in_=pb[:])
+        table_to_psum(0, 1)
+        flip_sign(2, POS_BLOCKS)
+
+        def pairs(ap):
+            return ap.rearrange("p (i e) -> p i e", e=2)
+
+        def project(c, n, mm):
+            xc = x_codes[c % X_BUFS]
+            xp = x_planes[c % X_BUFS]
+            acc = accs.tile([P, N_TILE], F32, name="acc")
+            for g in range(PASSES):
+                nc.tensor.matmul_mx(
+                    out=acc[:],
+                    lhsT=xc[:, g, 2 * P * mm : 2 * P * (mm + 1)].bitcast(FP4X4),
+                    lhsT_scale=xp[:, g, P * mm : P * (mm + 1)],
+                    rhs=w_codes[n][:, g, :].bitcast(FP4X4),
+                    rhs_scale=w_planes[n][:, g, :],
+                    start=(g == 0),
+                    stop=(g == PASSES - 1),
+                )
+            return acc
+
+        def epilogue(acc, m, n):
+            b = m // POS_BLOCKS
+            k = m % POS_BLOCKS
+            cos_p = tab_ps[k // 2][:, D * (k % 2) : D * (k % 2 + 1)]
+            sin_p = tab_ps[k // 2][:, 2 * D + D * (k % 2) : 2 * D + D * (k % 2 + 1)]
+            y = work.tile([P, N_TILE], F32, name="y")
+            t1 = work.tile([P, N_TILE], F32, name="t1")
+            t2 = work.tile([P, N_TILE], F32, name="t2")
+            z = work.tile([P, N_TILE], F32, name="z")
+            o = work.tile([P, N_TILE], F32, name="o")
+            heads = [slice(D * h, D * (h + 1)) for h in range(N_TILE // D)]
+            for sl in heads:
+                nc.vector.tensor_tensor(out=y[:, sl], in0=acc[:, sl], in1=bias_sb[:, N_TILE * n + sl.start : N_TILE * n + sl.stop], op=ADD)
+            for sl in heads:
+                nc.vector.tensor_tensor(out=t1[:, sl], in0=y[:, sl], in1=cos_p, op=MULT)
+            for sl in heads:
+                nc.vector.tensor_tensor(out=pairs(t2[:, sl]), in0=pairs(y[:, sl])[:, :, ::-1], in1=pairs(sin_p), op=MULT)
+            nc.gpsimd.tensor_tensor(out=z[:], in0=t1[:], in1=t2[:], op=ADD)
+            nc.scalar.activation(out=o[:], in_=z[:], func=RELU)
+            nc.scalar.dma_start(
+                out=out[b, 2 * n : 2 * n + 2, P * k : P * (k + 1), :].rearrange("h p d -> p h d"),
+                in_=o[:].rearrange("p (h d) -> p h d", d=D),
+            )
+
+        first = True
+        for c in range(N_CHUNKS):
+            for n in range(N_BLOCKS):
+                for mm in range(CHUNK_BLOCKS):
+                    acc = project(c, n, mm)
+                    if first:
+                        for j in range(1, POS_BLOCKS // 2):
+                            table_to_psum(j, 0)
+                            table_to_psum(j, 1)
+                        first = False
+                    epilogue(acc, CHUNK_BLOCKS * c + mm, n)
+            if c + X_BUFS < N_CHUNKS:
+                load_x_chunk(c + X_BUFS)

@@ -26,6 +26,7 @@ CHUNK_TOKENS = CHUNK_BLOCKS * P
 N_CHUNKS = B * S // CHUNK_TOKENS
 POS_BLOCKS = S // P
 X_BUFS = 2
+WARM_UP = 5
 
 
 def tile_lineartransformerblock_pa_kernel(tc, x_words, x_scales, cos, sin, Wq_words, Wq_scales, bq, out):
@@ -49,6 +50,7 @@ def tile_lineartransformerblock_pa_kernel(tc, x_words, x_scales, cos, sin, Wq_wo
             x_planes.append(keep.tile([P, PASSES, CHUNK_TOKENS], U8, name="x_planes%d" % j, align_bytes=64))
         brow = keep.tile([P, E], BF16, name="brow")
         ones = keep.tile([P, P], BF16, name="ones")
+        warm = keep.tile([P, N_TILE], BF16, name="warm")
         ident = keep.tile([P, P], BF16, name="ident")
         tab_sb = keep.tile([P, 2, POS_BLOCKS, D], BF16, name="tab_sb")
         bias_sb = keep.tile([P, E], F32, name="bias_sb")
@@ -62,59 +64,60 @@ def tile_lineartransformerblock_pa_kernel(tc, x_words, x_scales, cos, sin, Wq_wo
                 in_=src[g0:g1, :, col0 : col0 + ncols].rearrange("g p c -> p g c").bitcast(I32),
             )
 
-        def load_scales(dst, src, g0, g1, col0, ncols):
+        def load_scales(dst, src, col0, ncols, dcol0):
             for r in range(4):
                 nc.sync.dma_start(
-                    out=dst[r:P:32, g0:g1, :].bitcast(I32),
-                    in_=src[g0:g1, r:16:4, col0 : col0 + ncols].rearrange("g q n -> q g n").bitcast(I32),
+                    out=dst[r:P:32, :, dcol0 : dcol0 + ncols].bitcast(I32),
+                    in_=src[:, r:16:4, col0 : col0 + ncols].rearrange("g q n -> q g n").bitcast(I32),
                 )
 
         def load_x_chunk(c):
             j = c % X_BUFS
             load_codes(x_codes[j], x_words, 0, PASSES, 2 * CHUNK_TOKENS * c, 2 * CHUNK_TOKENS, 0)
-            load_scales(x_planes[j], x_scales, 0, PASSES, CHUNK_TOKENS * c, CHUNK_TOKENS)
+            load_scales(x_planes[j], x_scales, CHUNK_TOKENS * c, CHUNK_TOKENS, 0)
 
         def load_w_block(n):
             load_codes(w_codes[n], Wq_words, 0, PASSES, 2 * N_TILE * n, 2 * N_TILE, 0)
-            load_scales(w_planes[n], Wq_scales, 0, PASSES, N_TILE * n, N_TILE)
+            load_scales(w_planes[n], Wq_scales, N_TILE * n, N_TILE, 0)
 
         def zero_planes(t):
             nc.vector.memset(t[:].bitcast(I32), 0)
 
-        nc.vector.memset(brow[:], 0.0)
-        nc.vector.memset(ones[:], 1.0)
-        zero_planes(w_planes[0])
-        zero_planes(x_planes[0])
+        first_tokens = 2 * P
+        rest_tokens = CHUNK_TOKENS - first_tokens
+        nc.gpsimd.dma_start(out=tab_sb[:, 0, :, :], in_=cos.rearrange("(k p) d -> p k d", p=P))
+        nc.gpsimd.dma_start(out=tab_sb[:, 1, :, :], in_=sin.rearrange("(k p) d -> p k d", p=P))
         make_identity(nc, ident[:])
 
-        cos_v = cos.rearrange("(k p) d -> p k d", p=P)
-        sin_v = sin.rearrange("(k p) d -> p k d", p=P)
-        nc.scalar.dma_start(out=tab_sb[:, 0, 0:2, :], in_=cos_v[:, 0:2, :])
-        nc.scalar.dma_start(out=tab_sb[:, 1, 0:2, :], in_=sin_v[:, 0:2, :])
-        nc.scalar.dma_start(out=brow[0:1, :], in_=bq.rearrange("(o c) -> o c", o=1))
+        nc.vector.memset(warm[:], 0.0)
+        nc.vector.memset(x_planes[0][:, :, 0:first_tokens].bitcast(I32), 0)
+        nc.vector.memset(brow[:], 0.0)
+        zero_planes(w_planes[0])
+        nc.vector.memset(ones[:], 1.0)
+        nc.vector.memset(x_planes[0][:, :, first_tokens:CHUNK_TOKENS].bitcast(I32), 0)
 
-        half = PASSES // 2
-        load_codes(x_codes[0], x_words, 0, half, 0, 2 * CHUNK_TOKENS, 0)
-        load_codes(w_codes[0], Wq_words, 0, half, 0, 2 * N_TILE, 0)
-        load_scales(w_planes[0], Wq_scales, 0, PASSES, 0, N_TILE)
-        load_scales(x_planes[0], x_scales, 0, PASSES, 0, CHUNK_TOKENS)
-        load_codes(x_codes[0], x_words, half, PASSES, 0, 2 * CHUNK_TOKENS, 0)
-        load_codes(w_codes[0], Wq_words, half, PASSES, 0, 2 * N_TILE, 0)
-
-        nc.scalar.dma_start(out=tab_sb[:, 0, 2:POS_BLOCKS, :], in_=cos_v[:, 2:POS_BLOCKS, :])
-        nc.scalar.dma_start(out=tab_sb[:, 1, 2:POS_BLOCKS, :], in_=sin_v[:, 2:POS_BLOCKS, :])
+        load_scales(x_planes[0], x_scales, 0, first_tokens, 0)
+        load_codes(w_codes[0], Wq_words, 0, 2, 0, 2 * N_TILE, 0)
+        load_codes(x_codes[0], x_words, 0, 4, 0, 2 * first_tokens, 0)
+        nc.sync.dma_start(out=brow[0:1, :], in_=bq.rearrange("(o c) -> o c", o=1))
+        load_scales(w_planes[0], Wq_scales, 0, N_TILE, 0)
+        load_codes(w_codes[0], Wq_words, 2, 5, 0, 2 * N_TILE, 0)
+        load_codes(x_codes[0], x_words, 4, PASSES, 0, 2 * first_tokens, 0)
+        load_codes(w_codes[0], Wq_words, 5, PASSES, 0, 2 * N_TILE, 0)
+        load_codes(x_codes[0], x_words, 0, PASSES, 2 * first_tokens, 2 * rest_tokens, 2 * first_tokens)
+        load_scales(x_planes[0], x_scales, first_tokens, rest_tokens, first_tokens)
 
         for n in range(1, N_BLOCKS):
             zero_planes(w_planes[n])
         zero_planes(x_planes[1])
         load_w_block(1)
-        load_x_chunk(1)
         load_w_block(2)
         load_w_block(3)
+        load_x_chunk(1)
 
-        def flip_sign(k0, k1):
-            even = tab_sb[:, 1, k0:k1, :].rearrange("p k (i e) -> p k i e", e=2)[:, :, :, 0:1]
-            nc.scalar.activation(out=even, in_=even, func=COPY, scale=-1.0)
+        dummy = accs.tile([P, N_TILE], F32, name="acc")
+        for i in range(WARM_UP):
+            nc.tensor.matmul(dummy[:], lhsT=warm[:, 0:P], rhs=warm[:], start=True, stop=True)
 
         def table_to_psum(j, t):
             nc.tensor.matmul(
@@ -125,68 +128,111 @@ def tile_lineartransformerblock_pa_kernel(tc, x_words, x_scales, cos, sin, Wq_wo
                 stop=True,
             )
 
-        flip_sign(0, 2)
-        table_to_psum(0, 0)
+        for j in range(POS_BLOCKS // 2):
+            table_to_psum(j, 0)
+        even = tab_sb[:, 1, :, :].rearrange("p k (i e) -> p k i e", e=2)[:, :, :, 0:1]
+        nc.scalar.activation(out=even, in_=even, func=COPY, scale=-1.0)
         for n in range(N_BLOCKS):
             pb = accs.tile([P, N_TILE], F32, name="acc")
             nc.tensor.matmul(pb[:], lhsT=ones[:], rhs=brow[:, N_TILE * n : N_TILE * (n + 1)], start=True, stop=True)
             nc.scalar.copy(out=bias_sb[:, N_TILE * n : N_TILE * (n + 1)], in_=pb[:])
-        table_to_psum(0, 1)
-        flip_sign(2, POS_BLOCKS)
+        for j in range(POS_BLOCKS // 2):
+            table_to_psum(j, 1)
 
         def pairs(ap):
             return ap.rearrange("p (i e) -> p i e", e=2)
 
-        def project(c, n, mm):
+        def project(c, mm, ch0, width):
             xc = x_codes[c % X_BUFS]
             xp = x_planes[c % X_BUFS]
+            n = ch0 // N_TILE
+            lo = ch0 % N_TILE
             acc = accs.tile([P, N_TILE], F32, name="acc")
             for g in range(PASSES):
                 nc.tensor.matmul_mx(
-                    out=acc[:],
+                    out=acc[:, 0:width],
                     lhsT=xc[:, g, 2 * P * mm : 2 * P * (mm + 1)].bitcast(FP4X4),
                     lhsT_scale=xp[:, g, P * mm : P * (mm + 1)],
-                    rhs=w_codes[n][:, g, :].bitcast(FP4X4),
-                    rhs_scale=w_planes[n][:, g, :],
+                    rhs=w_codes[n][:, g, 2 * lo : 2 * (lo + width)].bitcast(FP4X4),
+                    rhs_scale=w_planes[n][:, g, lo : lo + width],
                     start=(g == 0),
                     stop=(g == PASSES - 1),
                 )
             return acc
 
-        def epilogue(acc, m, n):
-            b = m // POS_BLOCKS
-            k = m % POS_BLOCKS
-            cos_p = tab_ps[k // 2][:, D * (k % 2) : D * (k % 2 + 1)]
-            sin_p = tab_ps[k // 2][:, 2 * D + D * (k % 2) : 2 * D + D * (k % 2 + 1)]
-            y = work.tile([P, N_TILE], F32, name="y")
-            t1 = work.tile([P, N_TILE], F32, name="t1")
-            t2 = work.tile([P, N_TILE], F32, name="t2")
-            z = work.tile([P, N_TILE], F32, name="z")
-            o = work.tile([P, N_TILE], F32, name="o")
-            heads = [slice(D * h, D * (h + 1)) for h in range(N_TILE // D)]
-            for sl in heads:
-                nc.vector.tensor_tensor(out=y[:, sl], in0=acc[:, sl], in1=bias_sb[:, N_TILE * n + sl.start : N_TILE * n + sl.stop], op=ADD)
-            for sl in heads:
-                nc.vector.tensor_tensor(out=t1[:, sl], in0=y[:, sl], in1=cos_p, op=MULT)
-            for sl in heads:
-                nc.vector.tensor_tensor(out=pairs(t2[:, sl]), in0=pairs(y[:, sl])[:, :, ::-1], in1=pairs(sin_p), op=MULT)
-            nc.gpsimd.tensor_tensor(out=z[:], in0=t1[:], in1=t2[:], op=ADD)
-            nc.scalar.activation(out=o[:], in_=z[:], func=RELU)
-            nc.scalar.dma_start(
-                out=out[b, 2 * n : 2 * n + 2, P * k : P * (k + 1), :].rearrange("h p d -> p h d"),
-                in_=o[:].rearrange("p (h d) -> p h d", d=D),
+        def new_job(m, ch0):
+            job = {"m": m, "ch0": ch0}
+            for nm in ("y", "t1", "t2", "z", "o"):
+                job[nm] = work.tile([P, N_TILE], F32, name=nm)
+            return job
+
+        def table(job, t, lo, hi):
+            k = job["m"] % POS_BLOCKS
+            d0 = 2 * D * t + D * (k % 2) + (job["ch0"] + lo) % D
+            return tab_ps[k // 2][:, d0 : d0 + hi - lo]
+
+        def add_bias(job, acc, alo, lo, hi):
+            nc.vector.tensor_tensor(
+                out=job["y"][:, lo:hi], in0=acc[:, alo : alo + hi - lo], in1=bias_sb[:, job["ch0"] + lo : job["ch0"] + hi], op=ADD
             )
 
-        first = True
-        for c in range(N_CHUNKS):
-            for n in range(N_BLOCKS):
-                for mm in range(CHUNK_BLOCKS):
-                    acc = project(c, n, mm)
-                    if first:
-                        for j in range(1, POS_BLOCKS // 2):
-                            table_to_psum(j, 0)
-                            table_to_psum(j, 1)
-                        first = False
-                    epilogue(acc, CHUNK_BLOCKS * c + mm, n)
-            if c + X_BUFS < N_CHUNKS:
+        def times_cos(job, lo, hi):
+            nc.vector.tensor_tensor(out=job["t1"][:, lo:hi], in0=job["y"][:, lo:hi], in1=table(job, 0, lo, hi), op=MULT)
+
+        def times_sin(job, lo, hi):
+            nc.vector.tensor_tensor(
+                out=pairs(job["t2"][:, lo:hi]), in0=pairs(job["y"][:, lo:hi])[:, :, ::-1], in1=pairs(table(job, 1, lo, hi)), op=MULT
+            )
+
+        def add_terms(eng, job, lo, hi):
+            eng.tensor_tensor(out=job["z"][:, lo:hi], in0=job["t1"][:, lo:hi], in1=job["t2"][:, lo:hi], op=ADD)
+
+        def relu_store(job, width):
+            b = job["m"] // POS_BLOCKS
+            k = job["m"] % POS_BLOCKS
+            h0 = job["ch0"] // D
+            nc.scalar.activation(out=job["o"][:, 0:width], in_=job["z"][:, 0:width], func=RELU)
+            nc.scalar.dma_start(
+                out=out[b, h0 : h0 + width // D, P * k : P * (k + 1), :].rearrange("h p d -> p h d"),
+                in_=job["o"][:, 0:width].rearrange("p (h d) -> p h d", d=D),
+            )
+
+        def vector_part(job, pieces, step):
+            spans = [(lo, lo + step) for lo in range(0, step * len(pieces), step)]
+            for (acc, alo), (lo, hi) in zip(pieces, spans):
+                add_bias(job, acc, alo, lo, hi)
+            for lo, hi in spans:
+                times_cos(job, lo, hi)
+            for lo, hi in spans:
+                times_sin(job, lo, hi)
+
+        tiles = [(c, n, mm) for c in range(N_CHUNKS) for n in range(N_BLOCKS) for mm in range(CHUNK_BLOCKS)]
+
+        def epilogue(acc, c, n, mm):
+            job = new_job(CHUNK_BLOCKS * c + mm, N_TILE * n)
+            vector_part(job, [(acc, 0), (acc, D)], D)
+            add_terms(nc.gpsimd, job, 0, N_TILE)
+            relu_store(job, N_TILE)
+
+        waiting = []
+        for i, (c, n, mm) in enumerate(tiles[:-1]):
+            waiting.append((project(c, mm, N_TILE * n, N_TILE), c, n, mm))
+            if n == N_BLOCKS - 1 and mm == CHUNK_BLOCKS - 1 and c + X_BUFS < N_CHUNKS:
                 load_x_chunk(c + X_BUFS)
+            if i >= 1:
+                epilogue(*waiting.pop(0))
+        epilogue(*waiting.pop(0))
+
+        c, n, mm = tiles[-1]
+        m = CHUNK_BLOCKS * c + mm
+        acc_a = project(c, mm, N_TILE * n, D)
+        acc_b = project(c, mm, N_TILE * n + D, D // 2)
+        acc_c = project(c, mm, N_TILE * n + D + D // 2, D // 2)
+        job_a = new_job(m, N_TILE * n)
+        job_b = new_job(m, N_TILE * n + D)
+        vector_part(job_a, [(acc_a, 0), (acc_a, D // 2)], D // 2)
+        add_terms(nc.gpsimd, job_a, 0, D)
+        vector_part(job_b, [(acc_b, 0), (acc_c, 0)], D // 2)
+        add_terms(nc.vector, job_b, 0, D)
+        relu_store(job_a, D)
+        relu_store(job_b, D)

@@ -26,7 +26,6 @@ CHUNK_TOKENS = CHUNK_BLOCKS * P
 N_CHUNKS = B * S // CHUNK_TOKENS
 POS_BLOCKS = S // P
 X_BUFS = 2
-WARM_UP = 5
 
 
 def tile_lineartransformerblock_pa_kernel(tc, x_words, x_scales, cos, sin, Wq_words, Wq_scales, bq, out):
@@ -50,7 +49,6 @@ def tile_lineartransformerblock_pa_kernel(tc, x_words, x_scales, cos, sin, Wq_wo
             x_planes.append(keep.tile([P, PASSES, CHUNK_TOKENS], U8, name="x_planes%d" % j, align_bytes=64))
         brow = keep.tile([P, E], BF16, name="brow")
         ones = keep.tile([P, P], BF16, name="ones")
-        warm = keep.tile([P, N_TILE], BF16, name="warm")
         ident = keep.tile([P, P], BF16, name="ident")
         tab_sb = keep.tile([P, 2, POS_BLOCKS, D], BF16, name="tab_sb")
         bias_sb = keep.tile([P, E], F32, name="bias_sb")
@@ -80,44 +78,8 @@ def tile_lineartransformerblock_pa_kernel(tc, x_words, x_scales, cos, sin, Wq_wo
             load_codes(w_codes[n], Wq_words, 0, PASSES, 2 * N_TILE * n, 2 * N_TILE, 0)
             load_scales(w_planes[n], Wq_scales, N_TILE * n, N_TILE, 0)
 
-        def zero_planes(t):
-            nc.vector.memset(t[:].bitcast(I32), 0)
-
-        first_tokens = 2 * P
-        rest_tokens = CHUNK_TOKENS - first_tokens
-        nc.gpsimd.dma_start(out=tab_sb[:, 0, :, :], in_=cos.rearrange("(k p) d -> p k d", p=P))
-        nc.gpsimd.dma_start(out=tab_sb[:, 1, :, :], in_=sin.rearrange("(k p) d -> p k d", p=P))
-        make_identity(nc, ident[:])
-
-        nc.vector.memset(warm[:], 0.0)
-        nc.vector.memset(x_planes[0][:, :, 0:first_tokens].bitcast(I32), 0)
-        nc.vector.memset(brow[:], 0.0)
-        zero_planes(w_planes[0])
-        nc.vector.memset(ones[:], 1.0)
-        nc.vector.memset(x_planes[0][:, :, first_tokens:CHUNK_TOKENS].bitcast(I32), 0)
-
-        load_scales(x_planes[0], x_scales, 0, first_tokens, 0)
-        load_codes(w_codes[0], Wq_words, 0, 2, 0, 2 * N_TILE, 0)
-        load_codes(x_codes[0], x_words, 0, 4, 0, 2 * first_tokens, 0)
-        nc.sync.dma_start(out=brow[0:1, :], in_=bq.rearrange("(o c) -> o c", o=1))
-        load_scales(w_planes[0], Wq_scales, 0, N_TILE, 0)
-        load_codes(w_codes[0], Wq_words, 2, 5, 0, 2 * N_TILE, 0)
-        load_codes(x_codes[0], x_words, 4, PASSES, 0, 2 * first_tokens, 0)
-        load_codes(w_codes[0], Wq_words, 5, PASSES, 0, 2 * N_TILE, 0)
-        load_codes(x_codes[0], x_words, 0, PASSES, 2 * first_tokens, 2 * rest_tokens, 2 * first_tokens)
-        load_scales(x_planes[0], x_scales, first_tokens, rest_tokens, first_tokens)
-
-        for n in range(1, N_BLOCKS):
-            zero_planes(w_planes[n])
-        zero_planes(x_planes[1])
-        load_w_block(1)
-        load_w_block(2)
-        load_w_block(3)
-        load_x_chunk(1)
-
-        dummy = accs.tile([P, N_TILE], F32, name="acc")
-        for i in range(WARM_UP):
-            nc.tensor.matmul(dummy[:], lhsT=warm[:, 0:P], rhs=warm[:], start=True, stop=True)
+        def zero_planes(ap):
+            nc.vector.memset(ap.bitcast(I32), 0)
 
         def table_to_psum(j, t):
             nc.tensor.matmul(
@@ -128,16 +90,45 @@ def tile_lineartransformerblock_pa_kernel(tc, x_words, x_scales, cos, sin, Wq_wo
                 stop=True,
             )
 
+        first_tokens = 2 * P
+        rest_tokens = CHUNK_TOKENS - first_tokens
+        make_identity(nc, ident[:])
+        zero_planes(x_planes[0][:, :, 0:first_tokens])
+        nc.vector.memset(brow[:], 0.0)
+        zero_planes(w_planes[0][:])
+        nc.vector.memset(ones[:], 1.0)
+        zero_planes(x_planes[0][:, :, first_tokens:CHUNK_TOKENS])
+        zero_planes(w_planes[1][:])
+
+        load_codes(w_codes[0], Wq_words, 0, 2, 0, 2 * N_TILE, 0)
+        load_scales(x_planes[0], x_scales, 0, first_tokens, 0)
+        nc.sync.dma_start(out=brow[0:1, :], in_=bq.rearrange("(o c) -> o c", o=1))
+        nc.sync.dma_start(out=tab_sb[:, 0, :, :], in_=cos.rearrange("(k p) d -> p k d", p=P))
+        nc.sync.dma_start(out=tab_sb[:, 1, :, :], in_=sin.rearrange("(k p) d -> p k d", p=P))
+        load_scales(w_planes[0], Wq_scales, 0, N_TILE, 0)
+        load_codes(x_codes[0], x_words, 0, PASSES, 0, 2 * first_tokens, 0)
+        load_codes(w_codes[0], Wq_words, 2, 5, 0, 2 * N_TILE, 0)
+        load_codes(w_codes[0], Wq_words, 5, PASSES, 0, 2 * N_TILE, 0)
+        load_codes(x_codes[0], x_words, 0, PASSES, 2 * first_tokens, 2 * rest_tokens, 2 * first_tokens)
+        load_scales(x_planes[0], x_scales, first_tokens, rest_tokens, first_tokens)
+        load_w_block(1)
+
+        for n in range(N_BLOCKS):
+            pb = accs.tile([P, N_TILE], F32, name="acc")
+            nc.tensor.matmul(pb[:], lhsT=ones[:], rhs=brow[:, N_TILE * n : N_TILE * (n + 1)], start=True, stop=True)
+            nc.vector.tensor_copy(out=bias_sb[:, N_TILE * n : N_TILE * (n + 1)], in_=pb[:])
         for j in range(POS_BLOCKS // 2):
             table_to_psum(j, 0)
         even = tab_sb[:, 1, :, :].rearrange("p k (i e) -> p k i e", e=2)[:, :, :, 0:1]
         nc.scalar.activation(out=even, in_=even, func=COPY, scale=-1.0)
-        for n in range(N_BLOCKS):
-            pb = accs.tile([P, N_TILE], F32, name="acc")
-            nc.tensor.matmul(pb[:], lhsT=ones[:], rhs=brow[:, N_TILE * n : N_TILE * (n + 1)], start=True, stop=True)
-            nc.scalar.copy(out=bias_sb[:, N_TILE * n : N_TILE * (n + 1)], in_=pb[:])
         for j in range(POS_BLOCKS // 2):
             table_to_psum(j, 1)
+
+        for n in range(2, N_BLOCKS):
+            zero_planes(w_planes[n][:])
+            load_w_block(n)
+        zero_planes(x_planes[1][:])
+        load_x_chunk(1)
 
         def pairs(ap):
             return ap.rearrange("p (i e) -> p i e", e=2)
@@ -160,79 +151,77 @@ def tile_lineartransformerblock_pa_kernel(tc, x_words, x_scales, cos, sin, Wq_wo
                 )
             return acc
 
-        def new_job(m, ch0):
-            job = {"m": m, "ch0": ch0}
-            for nm in ("y", "t1", "t2", "z", "o"):
-                job[nm] = work.tile([P, N_TILE], F32, name=nm)
-            return job
+        def tensor_part(c, mm, ch0, widths, span):
+            spans = []
+            for width in widths:
+                acc = project(c, mm, ch0, width)
+                spans.extend([(acc, lo) for lo in range(0, width, span)])
+                ch0 += width
+            return spans
 
-        def table(job, t, lo, hi):
-            k = job["m"] % POS_BLOCKS
-            d0 = 2 * D * t + D * (k % 2) + (job["ch0"] + lo) % D
-            return tab_ps[k // 2][:, d0 : d0 + hi - lo]
+        def rest_of_job(spans, c, mm, ch0, span, adder):
+            m = CHUNK_BLOCKS * c + mm
+            b = m // POS_BLOCKS
+            k = m % POS_BLOCKS
+            total = span * len(spans)
+            y = work.tile([P, N_TILE], F32, name="y")
+            t1 = work.tile([P, N_TILE], F32, name="t1")
+            t2 = work.tile([P, N_TILE], F32, name="t2")
+            z = work.tile([P, N_TILE], F32, name="z")
+            o = work.tile([P, N_TILE], F32, name="o")
+            cols = [slice(lo, lo + span) for lo in range(0, total, span)]
 
-        def add_bias(job, acc, alo, lo, hi):
-            nc.vector.tensor_tensor(
-                out=job["y"][:, lo:hi], in0=acc[:, alo : alo + hi - lo], in1=bias_sb[:, job["ch0"] + lo : job["ch0"] + hi], op=ADD
-            )
+            def table(t, sl):
+                d0 = 2 * D * t + D * (k % 2) + (ch0 + sl.start) % D
+                return tab_ps[k // 2][:, d0 : d0 + span]
 
-        def times_cos(job, lo, hi):
-            nc.vector.tensor_tensor(out=job["t1"][:, lo:hi], in0=job["y"][:, lo:hi], in1=table(job, 0, lo, hi), op=MULT)
+            def add_bias(acc, lo, sl):
+                nc.vector.tensor_tensor(
+                    out=y[:, sl], in0=acc[:, lo : lo + span], in1=bias_sb[:, ch0 + sl.start : ch0 + sl.stop], op=ADD
+                )
 
-        def times_sin(job, lo, hi):
-            nc.vector.tensor_tensor(
-                out=pairs(job["t2"][:, lo:hi]), in0=pairs(job["y"][:, lo:hi])[:, :, ::-1], in1=pairs(table(job, 1, lo, hi)), op=MULT
-            )
+            def times_cos(sl):
+                nc.vector.tensor_tensor(out=t1[:, sl], in0=y[:, sl], in1=table(0, sl), op=MULT)
 
-        def add_terms(eng, job, lo, hi):
-            eng.tensor_tensor(out=job["z"][:, lo:hi], in0=job["t1"][:, lo:hi], in1=job["t2"][:, lo:hi], op=ADD)
+            def times_sin(sl):
+                nc.vector.tensor_tensor(out=pairs(t2[:, sl]), in0=pairs(y[:, sl])[:, :, ::-1], in1=pairs(table(1, sl)), op=MULT)
 
-        def relu_store(job, width):
-            b = job["m"] // POS_BLOCKS
-            k = job["m"] % POS_BLOCKS
-            h0 = job["ch0"] // D
-            nc.scalar.activation(out=job["o"][:, 0:width], in_=job["z"][:, 0:width], func=RELU)
+            if adder is nc.vector:
+                for (acc, lo), sl in zip(spans, cols):
+                    add_bias(acc, lo, sl)
+                    times_cos(sl)
+                    times_sin(sl)
+            else:
+                for (acc, lo), sl in zip(spans, cols):
+                    add_bias(acc, lo, sl)
+                for sl in cols:
+                    times_cos(sl)
+                for sl in cols:
+                    times_sin(sl)
+            adder.tensor_tensor(out=z[:, 0:total], in0=t1[:, 0:total], in1=t2[:, 0:total], op=ADD)
+            nc.scalar.activation(out=o[:, 0:total], in_=z[:, 0:total], func=RELU)
             nc.scalar.dma_start(
-                out=out[b, h0 : h0 + width // D, P * k : P * (k + 1), :].rearrange("h p d -> p h d"),
-                in_=job["o"][:, 0:width].rearrange("p (h d) -> p h d", d=D),
+                out=out[b, ch0 // D : (ch0 + total) // D, P * k : P * (k + 1), :].rearrange("h p d -> p h d"),
+                in_=o[:, 0:total].rearrange("p (h d) -> p h d", d=D),
             )
 
-        def vector_part(job, pieces, step):
-            spans = [(lo, lo + step) for lo in range(0, step * len(pieces), step)]
-            for (acc, alo), (lo, hi) in zip(pieces, spans):
-                add_bias(job, acc, alo, lo, hi)
-            for lo, hi in spans:
-                times_cos(job, lo, hi)
-            for lo, hi in spans:
-                times_sin(job, lo, hi)
+        jobs = []
+        for c in range(N_CHUNKS):
+            for n in range(N_BLOCKS):
+                for mm in range(CHUNK_BLOCKS):
+                    jobs.append((c, mm, N_TILE * n, [N_TILE], D, nc.gpsimd))
+        c, mm, ch0 = jobs[-1][0:3]
+        jobs[-1:] = [
+            (c, mm, ch0, [D], D // 2, nc.gpsimd),
+            (c, mm, ch0 + D, [D // 2, D // 2], D // 2, nc.vector),
+        ]
 
-        tiles = [(c, n, mm) for c in range(N_CHUNKS) for n in range(N_BLOCKS) for mm in range(CHUNK_BLOCKS)]
-
-        def epilogue(acc, c, n, mm):
-            job = new_job(CHUNK_BLOCKS * c + mm, N_TILE * n)
-            vector_part(job, [(acc, 0), (acc, D)], D)
-            add_terms(nc.gpsimd, job, 0, N_TILE)
-            relu_store(job, N_TILE)
-
-        waiting = []
-        for i, (c, n, mm) in enumerate(tiles[:-1]):
-            waiting.append((project(c, mm, N_TILE * n, N_TILE), c, n, mm))
-            if n == N_BLOCKS - 1 and mm == CHUNK_BLOCKS - 1 and c + X_BUFS < N_CHUNKS:
+        ahead = None
+        for i, (c, mm, ch0, widths, span, adder) in enumerate(jobs):
+            spans = tensor_part(c, mm, ch0, widths, span)
+            if i + 1 < len(jobs) and jobs[i + 1][0] != c and c + X_BUFS < N_CHUNKS:
                 load_x_chunk(c + X_BUFS)
-            if i >= 1:
-                epilogue(*waiting.pop(0))
-        epilogue(*waiting.pop(0))
-
-        c, n, mm = tiles[-1]
-        m = CHUNK_BLOCKS * c + mm
-        acc_a = project(c, mm, N_TILE * n, D)
-        acc_b = project(c, mm, N_TILE * n + D, D // 2)
-        acc_c = project(c, mm, N_TILE * n + D + D // 2, D // 2)
-        job_a = new_job(m, N_TILE * n)
-        job_b = new_job(m, N_TILE * n + D)
-        vector_part(job_a, [(acc_a, 0), (acc_a, D // 2)], D // 2)
-        add_terms(nc.gpsimd, job_a, 0, D)
-        vector_part(job_b, [(acc_b, 0), (acc_c, 0)], D // 2)
-        add_terms(nc.vector, job_b, 0, D)
-        relu_store(job_a, D)
-        relu_store(job_b, D)
+            if ahead is not None:
+                rest_of_job(*ahead)
+            ahead = (spans, c, mm, ch0, span, adder)
+        rest_of_job(*ahead)

@@ -62,24 +62,52 @@ def tile_lineartransformerblock_pa_kernel(tc, x_words, x_scales, cos, sin, Wq_wo
                 in_=src[g0:g1, :, col0 : col0 + ncols].rearrange("g p c -> p g c").bitcast(I32),
             )
 
-        def load_scales(dst, src, col0, ncols, dcol0):
+        def load_scales(dst, src, g0, g1, col0, ncols):
             for r in range(4):
                 nc.sync.dma_start(
-                    out=dst[r:P:32, :, dcol0 : dcol0 + ncols].bitcast(I32),
-                    in_=src[:, r:16:4, col0 : col0 + ncols].rearrange("g q n -> q g n").bitcast(I32),
+                    out=dst[r:P:32, g0:g1, :].bitcast(I32),
+                    in_=src[g0:g1, r:16:4, col0 : col0 + ncols].rearrange("g q n -> q g n").bitcast(I32),
                 )
 
         def load_x_chunk(c):
             j = c % X_BUFS
             load_codes(x_codes[j], x_words, 0, PASSES, 2 * CHUNK_TOKENS * c, 2 * CHUNK_TOKENS, 0)
-            load_scales(x_planes[j], x_scales, CHUNK_TOKENS * c, CHUNK_TOKENS, 0)
+            load_scales(x_planes[j], x_scales, 0, PASSES, CHUNK_TOKENS * c, CHUNK_TOKENS)
 
         def load_w_block(n):
             load_codes(w_codes[n], Wq_words, 0, PASSES, 2 * N_TILE * n, 2 * N_TILE, 0)
-            load_scales(w_planes[n], Wq_scales, N_TILE * n, N_TILE, 0)
+            load_scales(w_planes[n], Wq_scales, 0, PASSES, N_TILE * n, N_TILE)
 
-        def zero_planes(ap):
-            nc.vector.memset(ap.bitcast(I32), 0)
+        def zero_planes(t):
+            nc.vector.memset(t[:].bitcast(I32), 0)
+
+        nc.vector.memset(brow[:], 0.0)
+        nc.vector.memset(ones[:], 1.0)
+        zero_planes(w_planes[0])
+        zero_planes(x_planes[0])
+        make_identity(nc, ident[:])
+
+        cos_v = cos.rearrange("(k p) d -> p k d", p=P)
+        sin_v = sin.rearrange("(k p) d -> p k d", p=P)
+        nc.scalar.dma_start(out=tab_sb[:, 0, 0:2, :], in_=cos_v[:, 0:2, :])
+        nc.scalar.dma_start(out=tab_sb[:, 1, 0:2, :], in_=sin_v[:, 0:2, :])
+        nc.scalar.dma_start(out=brow[0:1, :], in_=bq.rearrange("(o c) -> o c", o=1))
+
+        half = PASSES // 2
+        load_codes(x_codes[0], x_words, 0, half, 0, 2 * CHUNK_TOKENS, 0)
+        load_codes(w_codes[0], Wq_words, 0, half, 0, 2 * N_TILE, 0)
+        load_scales(w_planes[0], Wq_scales, 0, PASSES, 0, N_TILE)
+        load_scales(x_planes[0], x_scales, 0, PASSES, 0, CHUNK_TOKENS)
+        load_codes(x_codes[0], x_words, half, PASSES, 0, 2 * CHUNK_TOKENS, 0)
+        load_codes(w_codes[0], Wq_words, half, PASSES, 0, 2 * N_TILE, 0)
+
+        nc.scalar.dma_start(out=tab_sb[:, 0, 2:POS_BLOCKS, :], in_=cos_v[:, 2:POS_BLOCKS, :])
+        nc.scalar.dma_start(out=tab_sb[:, 1, 2:POS_BLOCKS, :], in_=sin_v[:, 2:POS_BLOCKS, :])
+
+
+        def flip_sign(k0, k1):
+            even = tab_sb[:, 1, k0:k1, :].rearrange("p k (i e) -> p k i e", e=2)[:, :, :, 0:1]
+            nc.scalar.activation(out=even, in_=even, func=COPY, scale=-1.0)
 
         def table_to_psum(j, t):
             nc.tensor.matmul(
@@ -90,138 +118,73 @@ def tile_lineartransformerblock_pa_kernel(tc, x_words, x_scales, cos, sin, Wq_wo
                 stop=True,
             )
 
-        first_tokens = 2 * P
-        rest_tokens = CHUNK_TOKENS - first_tokens
-        make_identity(nc, ident[:])
-        zero_planes(x_planes[0][:, :, 0:first_tokens])
-        nc.vector.memset(brow[:], 0.0)
-        zero_planes(w_planes[0][:])
-        nc.vector.memset(ones[:], 1.0)
-        zero_planes(x_planes[0][:, :, first_tokens:CHUNK_TOKENS])
-        zero_planes(w_planes[1][:])
-
-        load_codes(w_codes[0], Wq_words, 0, 2, 0, 2 * N_TILE, 0)
-        load_scales(x_planes[0], x_scales, 0, first_tokens, 0)
-        nc.sync.dma_start(out=brow[0:1, :], in_=bq.rearrange("(o c) -> o c", o=1))
-        nc.sync.dma_start(out=tab_sb[:, 0, :, :], in_=cos.rearrange("(k p) d -> p k d", p=P))
-        nc.sync.dma_start(out=tab_sb[:, 1, :, :], in_=sin.rearrange("(k p) d -> p k d", p=P))
-        load_scales(w_planes[0], Wq_scales, 0, N_TILE, 0)
-        load_codes(x_codes[0], x_words, 0, PASSES, 0, 2 * first_tokens, 0)
-        load_codes(w_codes[0], Wq_words, 2, 5, 0, 2 * N_TILE, 0)
-        load_codes(w_codes[0], Wq_words, 5, PASSES, 0, 2 * N_TILE, 0)
-        load_codes(x_codes[0], x_words, 0, PASSES, 2 * first_tokens, 2 * rest_tokens, 2 * first_tokens)
-        load_scales(x_planes[0], x_scales, first_tokens, rest_tokens, first_tokens)
-        load_w_block(1)
-
+        flip_sign(0, 2)
+        flip_sign(2, POS_BLOCKS)
+        table_to_psum(0, 0)
         for n in range(N_BLOCKS):
             pb = accs.tile([P, N_TILE], F32, name="acc")
             nc.tensor.matmul(pb[:], lhsT=ones[:], rhs=brow[:, N_TILE * n : N_TILE * (n + 1)], start=True, stop=True)
             nc.vector.tensor_copy(out=bias_sb[:, N_TILE * n : N_TILE * (n + 1)], in_=pb[:])
-        for j in range(POS_BLOCKS // 2):
+        table_to_psum(0, 1)
+        for j in range(1, POS_BLOCKS // 2):
             table_to_psum(j, 0)
-        even = tab_sb[:, 1, :, :].rearrange("p k (i e) -> p k i e", e=2)[:, :, :, 0:1]
-        nc.scalar.activation(out=even, in_=even, func=COPY, scale=-1.0)
-        for j in range(POS_BLOCKS // 2):
             table_to_psum(j, 1)
 
-        for n in range(2, N_BLOCKS):
-            zero_planes(w_planes[n][:])
-            load_w_block(n)
-        zero_planes(x_planes[1][:])
+        for n in range(1, N_BLOCKS):
+            zero_planes(w_planes[n])
+        zero_planes(x_planes[1])
+        load_w_block(1)
         load_x_chunk(1)
+        load_w_block(2)
+        load_w_block(3)
 
         def pairs(ap):
             return ap.rearrange("p (i e) -> p i e", e=2)
 
-        def project(c, mm, ch0, width):
+        def project(c, n, mm):
             xc = x_codes[c % X_BUFS]
             xp = x_planes[c % X_BUFS]
-            n = ch0 // N_TILE
-            lo = ch0 % N_TILE
             acc = accs.tile([P, N_TILE], F32, name="acc")
             for g in range(PASSES):
                 nc.tensor.matmul_mx(
-                    out=acc[:, 0:width],
+                    out=acc[:],
                     lhsT=xc[:, g, 2 * P * mm : 2 * P * (mm + 1)].bitcast(FP4X4),
                     lhsT_scale=xp[:, g, P * mm : P * (mm + 1)],
-                    rhs=w_codes[n][:, g, 2 * lo : 2 * (lo + width)].bitcast(FP4X4),
-                    rhs_scale=w_planes[n][:, g, lo : lo + width],
+                    rhs=w_codes[n][:, g, :].bitcast(FP4X4),
+                    rhs_scale=w_planes[n][:, g, :],
                     start=(g == 0),
                     stop=(g == PASSES - 1),
                 )
             return acc
 
-        def tensor_part(c, mm, ch0, widths, span):
-            spans = []
-            for width in widths:
-                acc = project(c, mm, ch0, width)
-                spans.extend([(acc, lo) for lo in range(0, width, span)])
-                ch0 += width
-            return spans
-
-        def rest_of_job(spans, c, mm, ch0, span, adder):
-            m = CHUNK_BLOCKS * c + mm
+        def epilogue(acc, m, n):
             b = m // POS_BLOCKS
             k = m % POS_BLOCKS
-            total = span * len(spans)
+            cos_p = tab_ps[k // 2][:, D * (k % 2) : D * (k % 2 + 1)]
+            sin_p = tab_ps[k // 2][:, 2 * D + D * (k % 2) : 2 * D + D * (k % 2 + 1)]
             y = work.tile([P, N_TILE], F32, name="y")
             t1 = work.tile([P, N_TILE], F32, name="t1")
             t2 = work.tile([P, N_TILE], F32, name="t2")
             z = work.tile([P, N_TILE], F32, name="z")
             o = work.tile([P, N_TILE], F32, name="o")
-            cols = [slice(lo, lo + span) for lo in range(0, total, span)]
-
-            def table(t, sl):
-                d0 = 2 * D * t + D * (k % 2) + (ch0 + sl.start) % D
-                return tab_ps[k // 2][:, d0 : d0 + span]
-
-            def add_bias(acc, lo, sl):
-                nc.vector.tensor_tensor(
-                    out=y[:, sl], in0=acc[:, lo : lo + span], in1=bias_sb[:, ch0 + sl.start : ch0 + sl.stop], op=ADD
-                )
-
-            def times_cos(sl):
-                nc.vector.tensor_tensor(out=t1[:, sl], in0=y[:, sl], in1=table(0, sl), op=MULT)
-
-            def times_sin(sl):
-                nc.vector.tensor_tensor(out=pairs(t2[:, sl]), in0=pairs(y[:, sl])[:, :, ::-1], in1=pairs(table(1, sl)), op=MULT)
-
-            if adder is nc.vector:
-                for (acc, lo), sl in zip(spans, cols):
-                    add_bias(acc, lo, sl)
-                    times_cos(sl)
-                    times_sin(sl)
-            else:
-                for (acc, lo), sl in zip(spans, cols):
-                    add_bias(acc, lo, sl)
-                for sl in cols:
-                    times_cos(sl)
-                for sl in cols:
-                    times_sin(sl)
-            adder.tensor_tensor(out=z[:, 0:total], in0=t1[:, 0:total], in1=t2[:, 0:total], op=ADD)
-            nc.scalar.activation(out=o[:, 0:total], in_=z[:, 0:total], func=RELU)
+            heads = [slice(D * h, D * (h + 1)) for h in range(N_TILE // D)]
+            for sl in heads:
+                nc.vector.tensor_tensor(out=y[:, sl], in0=acc[:, sl], in1=bias_sb[:, N_TILE * n + sl.start : N_TILE * n + sl.stop], op=ADD)
+            for sl in heads:
+                nc.vector.tensor_tensor(out=t1[:, sl], in0=y[:, sl], in1=cos_p, op=MULT)
+            for sl in heads:
+                nc.vector.tensor_tensor(out=pairs(t2[:, sl]), in0=pairs(y[:, sl])[:, :, ::-1], in1=pairs(sin_p), op=MULT)
+            nc.gpsimd.tensor_tensor(out=z[:], in0=t1[:], in1=t2[:], op=ADD)
+            nc.scalar.activation(out=o[:], in_=z[:], func=RELU)
             nc.scalar.dma_start(
-                out=out[b, ch0 // D : (ch0 + total) // D, P * k : P * (k + 1), :].rearrange("h p d -> p h d"),
-                in_=o[:, 0:total].rearrange("p (h d) -> p h d", d=D),
+                out=out[b, 2 * n : 2 * n + 2, P * k : P * (k + 1), :].rearrange("h p d -> p h d"),
+                in_=o[:].rearrange("p (h d) -> p h d", d=D),
             )
 
-        jobs = []
         for c in range(N_CHUNKS):
             for n in range(N_BLOCKS):
                 for mm in range(CHUNK_BLOCKS):
-                    jobs.append((c, mm, N_TILE * n, [N_TILE], D, nc.gpsimd))
-        c, mm, ch0 = jobs[-1][0:3]
-        jobs[-1:] = [
-            (c, mm, ch0, [D], D // 2, nc.gpsimd),
-            (c, mm, ch0 + D, [D // 2, D // 2], D // 2, nc.vector),
-        ]
-
-        ahead = None
-        for i, (c, mm, ch0, widths, span, adder) in enumerate(jobs):
-            spans = tensor_part(c, mm, ch0, widths, span)
-            if i + 1 < len(jobs) and jobs[i + 1][0] != c and c + X_BUFS < N_CHUNKS:
+                    acc = project(c, n, mm)
+                    epilogue(acc, CHUNK_BLOCKS * c + mm, n)
+            if c + X_BUFS < N_CHUNKS:
                 load_x_chunk(c + X_BUFS)
-            if ahead is not None:
-                rest_of_job(*ahead)
-            ahead = (spans, c, mm, ch0, span, adder)
-        rest_of_job(*ahead)

@@ -157,7 +157,7 @@ def tile_lineartransformerblock_pa_kernel(tc, x_words, x_scales, cos, sin, Wq_wo
                 )
             return acc
 
-        def epilogue(acc, m, n):
+        def epilogue(acc, m, n, last):
             b = m // POS_BLOCKS
             k = m % POS_BLOCKS
             cos_p = tab_ps[k // 2][:, D * (k % 2) : D * (k % 2 + 1)]
@@ -174,17 +174,21 @@ def tile_lineartransformerblock_pa_kernel(tc, x_words, x_scales, cos, sin, Wq_wo
                 nc.vector.tensor_tensor(out=t1[:, sl], in0=y[:, sl], in1=cos_p, op=MULT)
             for sl in heads:
                 nc.vector.tensor_tensor(out=pairs(t2[:, sl]), in0=pairs(y[:, sl])[:, :, ::-1], in1=pairs(sin_p), op=MULT)
-            nc.gpsimd.tensor_tensor(out=z[:], in0=t1[:], in1=t2[:], op=ADD)
-            nc.scalar.activation(out=o[:], in_=z[:], func=RELU)
-            nc.scalar.dma_start(
-                out=out[b, 2 * n : 2 * n + 2, P * k : P * (k + 1), :].rearrange("h p d -> p h d"),
-                in_=o[:].rearrange("p (h d) -> p h d", d=D),
-            )
+            adder = nc.vector if last else nc.gpsimd
+            for sl in heads if last else [slice(0, N_TILE)]:
+                adder.tensor_tensor(out=z[:, sl], in0=t1[:, sl], in1=t2[:, sl], op=ADD)
+                nc.scalar.activation(out=o[:, sl], in_=z[:, sl], func=RELU)
+                h0 = (N_TILE * n + sl.start) // D
+                h1 = (N_TILE * n + sl.stop) // D
+                nc.scalar.dma_start(
+                    out=out[b, h0:h1, P * k : P * (k + 1), :].rearrange("h p d -> p h d"),
+                    in_=o[:, sl].rearrange("p (h d) -> p h d", d=D),
+                )
 
         for c in range(N_CHUNKS):
             for n in range(N_BLOCKS):
                 for mm in range(CHUNK_BLOCKS):
                     acc = project(c, n, mm)
-                    epilogue(acc, CHUNK_BLOCKS * c + mm, n)
+                    epilogue(acc, CHUNK_BLOCKS * c + mm, n, (c, n, mm) == (N_CHUNKS - 1, N_BLOCKS - 1, CHUNK_BLOCKS - 1))
             if c + X_BUFS < N_CHUNKS:
                 load_x_chunk(c + X_BUFS)

@@ -26,6 +26,7 @@ CHUNK_TOKENS = CHUNK_BLOCKS * P
 N_CHUNKS = B * S // CHUNK_TOKENS
 POS_BLOCKS = S // P
 X_BUFS = 2
+N_WARM = 40
 
 
 def tile_lineartransformerblock_pa_kernel(tc, x_words, x_scales, cos, sin, Wq_words, Wq_scales, bq, out):
@@ -52,6 +53,7 @@ def tile_lineartransformerblock_pa_kernel(tc, x_words, x_scales, cos, sin, Wq_wo
         ident = keep.tile([P, P], BF16, name="ident")
         tab_sb = keep.tile([P, 2, POS_BLOCKS, D], BF16, name="tab_sb")
         bias_sb = keep.tile([P, E], F32, name="bias_sb")
+        scr = keep.tile([P, 1], F32, name="scr")
         tab_ps = []
         for j in range(POS_BLOCKS // 2):
             tab_ps.append(tabs.tile([P, 4 * D], BF16, name="tab_ps%d" % j))
@@ -81,29 +83,25 @@ def tile_lineartransformerblock_pa_kernel(tc, x_words, x_scales, cos, sin, Wq_wo
         def zero_planes(t):
             nc.vector.memset(t[:].bitcast(I32), 0)
 
-        nc.vector.memset(brow[:], 0.0)
-        nc.vector.memset(ones[:], 1.0)
         zero_planes(w_planes[0])
         zero_planes(x_planes[0])
+        nc.vector.memset(brow[:], 0.0)
+        nc.vector.memset(ones[:], 1.0)
         make_identity(nc, ident[:])
 
         cos_v = cos.rearrange("(k p) d -> p k d", p=P)
         sin_v = sin.rearrange("(k p) d -> p k d", p=P)
-        nc.scalar.dma_start(out=tab_sb[:, 0, 0:2, :], in_=cos_v[:, 0:2, :])
-        nc.scalar.dma_start(out=tab_sb[:, 1, 0:2, :], in_=sin_v[:, 0:2, :])
-        nc.scalar.dma_start(out=brow[0:1, :], in_=bq.rearrange("(o c) -> o c", o=1))
-
         half = PASSES // 2
         load_codes(x_codes[0], x_words, 0, half, 0, 2 * CHUNK_TOKENS, 0)
         load_codes(w_codes[0], Wq_words, 0, half, 0, 2 * N_TILE, 0)
         load_scales(w_planes[0], Wq_scales, 0, PASSES, 0, N_TILE)
+        nc.scalar.dma_start(out=tab_sb[:, 1, :, :], in_=sin_v)
+        nc.scalar.dma_start(out=tab_sb[:, 0, :, :], in_=cos_v)
         load_scales(x_planes[0], x_scales, 0, PASSES, 0, CHUNK_TOKENS)
+        nc.scalar.activation(out=scr[:], in_=ident[:, 0:1], func=RELU)
+        nc.scalar.dma_start(out=brow[0:1, :], in_=bq.rearrange("(o c) -> o c", o=1))
         load_codes(x_codes[0], x_words, half, PASSES, 0, 2 * CHUNK_TOKENS, 0)
         load_codes(w_codes[0], Wq_words, half, PASSES, 0, 2 * N_TILE, 0)
-
-        nc.scalar.dma_start(out=tab_sb[:, 0, 2:POS_BLOCKS, :], in_=cos_v[:, 2:POS_BLOCKS, :])
-        nc.scalar.dma_start(out=tab_sb[:, 1, 2:POS_BLOCKS, :], in_=sin_v[:, 2:POS_BLOCKS, :])
-
 
         def flip_sign(k0, k1):
             even = tab_sb[:, 1, k0:k1, :].rearrange("p k (i e) -> p k i e", e=2)[:, :, :, 0:1]
@@ -118,17 +116,17 @@ def tile_lineartransformerblock_pa_kernel(tc, x_words, x_scales, cos, sin, Wq_wo
                 stop=True,
             )
 
-        flip_sign(0, 2)
-        flip_sign(2, POS_BLOCKS)
-        table_to_psum(0, 0)
+        warm = accs.tile([P, N_TILE], F32, name="acc")
+        for r in range(N_WARM):
+            nc.tensor.matmul(warm[:, 0:P], lhsT=ident[:], rhs=ident[:], start=True, stop=True)
+        flip_sign(0, POS_BLOCKS)
+        for t in range(2):
+            for j in range(POS_BLOCKS // 2):
+                table_to_psum(j, t)
         for n in range(N_BLOCKS):
             pb = accs.tile([P, N_TILE], F32, name="acc")
             nc.tensor.matmul(pb[:], lhsT=ones[:], rhs=brow[:, N_TILE * n : N_TILE * (n + 1)], start=True, stop=True)
             nc.vector.tensor_copy(out=bias_sb[:, N_TILE * n : N_TILE * (n + 1)], in_=pb[:])
-        table_to_psum(0, 1)
-        for j in range(1, POS_BLOCKS // 2):
-            table_to_psum(j, 0)
-            table_to_psum(j, 1)
 
         for n in range(1, N_BLOCKS):
             zero_planes(w_planes[n])
@@ -141,11 +139,10 @@ def tile_lineartransformerblock_pa_kernel(tc, x_words, x_scales, cos, sin, Wq_wo
         def pairs(ap):
             return ap.rearrange("p (i e) -> p i e", e=2)
 
-        def project(c, n, mm):
+        def passes(acc, c, n, mm, g0, g1):
             xc = x_codes[c % X_BUFS]
             xp = x_planes[c % X_BUFS]
-            acc = accs.tile([P, N_TILE], F32, name="acc")
-            for g in range(PASSES):
+            for g in range(g0, g1):
                 nc.tensor.matmul_mx(
                     out=acc[:],
                     lhsT=xc[:, g, 2 * P * mm : 2 * P * (mm + 1)].bitcast(FP4X4),
@@ -155,6 +152,10 @@ def tile_lineartransformerblock_pa_kernel(tc, x_words, x_scales, cos, sin, Wq_wo
                     start=(g == 0),
                     stop=(g == PASSES - 1),
                 )
+
+        def project(c, n, mm):
+            acc = accs.tile([P, N_TILE], F32, name="acc")
+            passes(acc, c, n, mm, 0, PASSES)
             return acc
 
         def epilogue(acc, m, n, last):
@@ -185,10 +186,20 @@ def tile_lineartransformerblock_pa_kernel(tc, x_words, x_scales, cos, sin, Wq_wo
                     in_=o[:, sl].rearrange("p (h d) -> p h d", d=D),
                 )
 
+        first = []
+        for mm in range(CHUNK_BLOCKS):
+            first.append(accs.tile([P, N_TILE], F32, name="acc"))
+        for g in range(PASSES):
+            for mm in range(CHUNK_BLOCKS):
+                passes(first[mm], 0, 0, mm, g, g + 1)
+        for mm in range(CHUNK_BLOCKS):
+            epilogue(first[mm], mm, 0, False)
+
         for c in range(N_CHUNKS):
             for n in range(N_BLOCKS):
                 for mm in range(CHUNK_BLOCKS):
-                    acc = project(c, n, mm)
-                    epilogue(acc, CHUNK_BLOCKS * c + mm, n, (c, n, mm) == (N_CHUNKS - 1, N_BLOCKS - 1, CHUNK_BLOCKS - 1))
+                    if (c, n) != (0, 0):
+                        acc = project(c, n, mm)
+                        epilogue(acc, CHUNK_BLOCKS * c + mm, n, (c, n, mm) == (N_CHUNKS - 1, N_BLOCKS - 1, CHUNK_BLOCKS - 1))
             if c + X_BUFS < N_CHUNKS:
                 load_x_chunk(c + X_BUFS)

@@ -26,7 +26,7 @@ CHUNK_TOKENS = CHUNK_BLOCKS * P
 N_CHUNKS = B * S // CHUNK_TOKENS
 POS_BLOCKS = S // P
 X_BUFS = 2
-N_WARM = 40
+N_WARM = 16
 
 
 def tile_lineartransformerblock_pa_kernel(tc, x_words, x_scales, cos, sin, Wq_words, Wq_scales, bq, out):
@@ -54,6 +54,7 @@ def tile_lineartransformerblock_pa_kernel(tc, x_words, x_scales, cos, sin, Wq_wo
         tab_sb = keep.tile([P, 2, POS_BLOCKS, D], BF16, name="tab_sb")
         bias_sb = keep.tile([P, E], F32, name="bias_sb")
         scr = keep.tile([P, 1], F32, name="scr")
+        scr_in = keep.tile([P, 1], F32, name="scr_in")
         tab_ps = []
         for j in range(POS_BLOCKS // 2):
             tab_ps.append(tabs.tile([P, 4 * D], BF16, name="tab_ps%d" % j))
@@ -83,23 +84,26 @@ def tile_lineartransformerblock_pa_kernel(tc, x_words, x_scales, cos, sin, Wq_wo
         def zero_planes(t):
             nc.vector.memset(t[:].bitcast(I32), 0)
 
+        nc.gpsimd.memset(scr_in[:], 0.0)
         zero_planes(w_planes[0])
-        zero_planes(x_planes[0])
         nc.vector.memset(brow[:], 0.0)
         nc.vector.memset(ones[:], 1.0)
+        zero_planes(x_planes[0])
         make_identity(nc, ident[:])
 
         cos_v = cos.rearrange("(k p) d -> p k d", p=P)
         sin_v = sin.rearrange("(k p) d -> p k d", p=P)
         half = PASSES // 2
-        load_codes(x_codes[0], x_words, 0, half, 0, 2 * CHUNK_TOKENS, 0)
-        load_codes(w_codes[0], Wq_words, 0, half, 0, 2 * N_TILE, 0)
+        load_codes(x_codes[0], x_words, 0, 2, 0, 2 * CHUNK_TOKENS, 0)
+        load_codes(w_codes[0], Wq_words, 0, 2, 0, 2 * N_TILE, 0)
         load_scales(w_planes[0], Wq_scales, 0, PASSES, 0, N_TILE)
         nc.scalar.dma_start(out=tab_sb[:, 1, :, :], in_=sin_v)
         nc.scalar.dma_start(out=tab_sb[:, 0, :, :], in_=cos_v)
-        load_scales(x_planes[0], x_scales, 0, PASSES, 0, CHUNK_TOKENS)
-        nc.scalar.activation(out=scr[:], in_=ident[:, 0:1], func=RELU)
         nc.scalar.dma_start(out=brow[0:1, :], in_=bq.rearrange("(o c) -> o c", o=1))
+        nc.scalar.activation(out=scr[:], in_=scr_in[:], func=RELU)
+        load_scales(x_planes[0], x_scales, 0, PASSES, 0, CHUNK_TOKENS)
+        load_codes(x_codes[0], x_words, 2, half, 0, 2 * CHUNK_TOKENS, 0)
+        load_codes(w_codes[0], Wq_words, 2, half, 0, 2 * N_TILE, 0)
         load_codes(x_codes[0], x_words, half, PASSES, 0, 2 * CHUNK_TOKENS, 0)
         load_codes(w_codes[0], Wq_words, half, PASSES, 0, 2 * N_TILE, 0)
 
@@ -118,15 +122,15 @@ def tile_lineartransformerblock_pa_kernel(tc, x_words, x_scales, cos, sin, Wq_wo
 
         warm = accs.tile([P, N_TILE], F32, name="acc")
         for r in range(N_WARM):
-            nc.tensor.matmul(warm[:, 0:P], lhsT=ident[:], rhs=ident[:], start=True, stop=True)
-        flip_sign(0, POS_BLOCKS)
-        for t in range(2):
-            for j in range(POS_BLOCKS // 2):
-                table_to_psum(j, t)
+            nc.tensor.matmul(warm[:, 0:P], lhsT=ones[:], rhs=ones[:], start=True, stop=True)
         for n in range(N_BLOCKS):
             pb = accs.tile([P, N_TILE], F32, name="acc")
             nc.tensor.matmul(pb[:], lhsT=ones[:], rhs=brow[:, N_TILE * n : N_TILE * (n + 1)], start=True, stop=True)
             nc.vector.tensor_copy(out=bias_sb[:, N_TILE * n : N_TILE * (n + 1)], in_=pb[:])
+        flip_sign(0, POS_BLOCKS)
+        for t in range(2):
+            for j in range(POS_BLOCKS // 2):
+                table_to_psum(j, t)
 
         for n in range(1, N_BLOCKS):
             zero_planes(w_planes[n])

@@ -136,9 +136,9 @@ def tile_lineartransformerblock_pa_kernel(tc, x_words, x_scales, cos, sin, Wq_wo
             zero_planes(w_planes[n])
         zero_planes(x_planes[1])
         load_w_block(1)
-        load_x_chunk(1)
         load_w_block(2)
         load_w_block(3)
+        load_x_chunk(1)
 
         def pairs(ap):
             return ap.rearrange("p (i e) -> p i e", e=2)

@@ -85,9 +85,9 @@ def tile_lineartransformerblock_pa_kernel(tc, x_words, x_scales, cos, sin, Wq_wo
             nc.vector.memset(t[:].bitcast(I32), 0)
 
         nc.gpsimd.memset(scr_in[:], 0.0)
-        zero_planes(w_planes[0])
-        nc.vector.memset(brow[:], 0.0)
         nc.vector.memset(ones[:], 1.0)
+        zero_planes(w_planes[0])
+        nc.vector.memset(brow[:].bitcast(I32), 0)
         zero_planes(x_planes[0])
         make_identity(nc, ident[:])
 
@@ -97,8 +97,8 @@ def tile_lineartransformerblock_pa_kernel(tc, x_words, x_scales, cos, sin, Wq_wo
         load_codes(x_codes[0], x_words, 0, 2, 0, 2 * CHUNK_TOKENS, 0)
         load_codes(w_codes[0], Wq_words, 0, 2, 0, 2 * N_TILE, 0)
         load_scales(w_planes[0], Wq_scales, 0, PASSES, 0, N_TILE)
-        nc.scalar.dma_start(out=tab_sb[:, 1, :, :], in_=sin_v)
         nc.scalar.dma_start(out=tab_sb[:, 0, :, :], in_=cos_v)
+        nc.scalar.dma_start(out=tab_sb[:, 1, :, :], in_=sin_v)
         nc.scalar.dma_start(out=brow[0:1, :], in_=bq.rearrange("(o c) -> o c", o=1))
         nc.scalar.activation(out=scr[:], in_=scr_in[:], func=RELU)
         load_scales(x_planes[0], x_scales, 0, PASSES, 0, CHUNK_TOKENS)
@@ -123,14 +123,15 @@ def tile_lineartransformerblock_pa_kernel(tc, x_words, x_scales, cos, sin, Wq_wo
         warm = accs.tile([P, N_TILE], F32, name="acc")
         for r in range(N_WARM):
             nc.tensor.matmul(warm[:, 0:P], lhsT=ones[:], rhs=ones[:], start=True, stop=True)
+        for j in range(POS_BLOCKS // 2):
+            table_to_psum(j, 0)
         for n in range(N_BLOCKS):
             pb = accs.tile([P, N_TILE], F32, name="acc")
             nc.tensor.matmul(pb[:], lhsT=ones[:], rhs=brow[:, N_TILE * n : N_TILE * (n + 1)], start=True, stop=True)
             nc.vector.tensor_copy(out=bias_sb[:, N_TILE * n : N_TILE * (n + 1)], in_=pb[:])
-        flip_sign(0, POS_BLOCKS)
-        for t in range(2):
-            for j in range(POS_BLOCKS // 2):
-                table_to_psum(j, t)
+        for j in range(POS_BLOCKS // 2):
+            flip_sign(2 * j, 2 * j + 2)
+            table_to_psum(j, 1)
 
         for n in range(1, N_BLOCKS):
             zero_planes(w_planes[n])

@@ -183,10 +183,15 @@ def tile_lineartransformerblock_pa_kernel(tc, x_words, x_scales, cos, sin, Wq_wo
             adder = nc.vector if last else nc.gpsimd
             for sl in heads if last else [slice(0, N_TILE)]:
                 adder.tensor_tensor(out=z[:, sl], in0=t1[:, sl], in1=t2[:, sl], op=ADD)
-                nc.scalar.activation(out=o[:, sl], in_=z[:, sl], func=RELU)
+                final = last and sl.stop == N_TILE
+                if final:
+                    nc.vector.tensor_scalar_max(out=o[:, sl], in0=z[:, sl], scalar1=0.0)
+                else:
+                    nc.scalar.activation(out=o[:, sl], in_=z[:, sl], func=RELU)
                 h0 = (N_TILE * n + sl.start) // D
                 h1 = (N_TILE * n + sl.stop) // D
-                nc.scalar.dma_start(
+                queue = nc.sync if final else nc.scalar
+                queue.dma_start(
                     out=out[b, h0:h1, P * k : P * (k + 1), :].rearrange("h p d -> p h d"),
                     in_=o[:, sl].rearrange("p (h d) -> p h d", d=D),
                 )

from contextlib import ExitStack

import concourse.mybir as mybir
from concourse.masks import make_identity

B, S, C, H, D = 4, 768, 4096, 8, 256
E = H * D
FLOPS = 2 * B * S * C * E

F32 = mybir.dt.float32
BF16 = mybir.dt.bfloat16
U8 = mybir.dt.uint8
I32 = mybir.dt.int32
FP4X4 = mybir.dt.float4_e2m1fn_x4
ADD = mybir.AluOpType.add
MULT = mybir.AluOpType.mult
RELU = mybir.ActivationFunctionType.Relu
COPY = mybir.ActivationFunctionType.Copy

P = 128
PASSES = C // 512
N_TILE = 512
N_BLOCKS = E // N_TILE
CHUNK_BLOCKS = 4
CHUNK_TOKENS = CHUNK_BLOCKS * P
N_CHUNKS = B * S // CHUNK_TOKENS
POS_BLOCKS = S // P
X_BUFS = 2
N_WARM = 16


def tile_lineartransformerblock_pa_kernel(tc, x_words, x_scales, cos, sin, Wq_words, Wq_scales, bq, out):
    nc = tc.nc
    with ExitStack() as ctx:
        keep = ctx.enter_context(tc.tile_pool(name="keep", bufs=1))
        work = ctx.enter_context(tc.tile_pool(name="work", bufs=3))
        tabs = ctx.enter_context(tc.psum_pool(name="tabs", bufs=1))
        accs = ctx.enter_context(tc.psum_pool(name="accs", bufs=5))
        ctx.enter_context(tc.manual_schedule())

        w_codes = []
        w_planes = []
        for n in range(N_BLOCKS):
            w_codes.append(keep.tile([P, PASSES, 2 * N_TILE], U8, name="w_codes%d" % n, align_bytes=64))
            w_planes.append(keep.tile([P, PASSES, N_TILE], U8, name="w_planes%d" % n, align_bytes=64))
        x_codes = []
        x_planes = []
        for j in range(X_BUFS):
            x_codes.append(keep.tile([P, PASSES, 2 * CHUNK_TOKENS], U8, name="x_codes%d" % j, align_bytes=64))
            x_planes.append(keep.tile([P, PASSES, CHUNK_TOKENS], U8, name="x_planes%d" % j, align_bytes=64))
        brow = keep.tile([P, E], BF16, name="brow")
        ones = keep.tile([P, P], BF16, name="ones")
        ident = keep.tile([P, P], BF16, name="ident")
        tab_sb = keep.tile([P, 2, POS_BLOCKS, D], BF16, name="tab_sb")
        bias_sb = keep.tile([P, E], F32, name="bias_sb")
        scr = keep.tile([P, 1], F32, name="scr")
        scr_in = keep.tile([P, 1], F32, name="scr_in")
        tab_ps = []
        for j in range(POS_BLOCKS // 2):
            tab_ps.append(tabs.tile([P, 4 * D], BF16, name="tab_ps%d" % j))

        def load_codes(dst, src, g0, g1, col0, ncols, dcol0):
            nc.sync.dma_start(
                out=dst[:, g0:g1, dcol0 : dcol0 + ncols].bitcast(I32),
                in_=src[g0:g1, :, col0 : col0 + ncols].rearrange("g p c -> p g c").bitcast(I32),
            )

        def load_scales(dst, src, g0, g1, col0, ncols):
            for r in range(4):
                nc.sync.dma_start(
                    out=dst[r:P:32, g0:g1, :].bitcast(I32),
                    in_=src[g0:g1, r:16:4, col0 : col0 + ncols].rearrange("g q n -> q g n").bitcast(I32),
                )

        def load_x_chunk(c):
            j = c % X_BUFS
            load_codes(x_codes[j], x_words, 0, PASSES, 2 * CHUNK_TOKENS * c, 2 * CHUNK_TOKENS, 0)
            load_scales(x_planes[j], x_scales, 0, PASSES, CHUNK_TOKENS * c, CHUNK_TOKENS)

        def load_w_block(n):
            load_codes(w_codes[n], Wq_words, 0, PASSES, 2 * N_TILE * n, 2 * N_TILE, 0)
            load_scales(w_planes[n], Wq_scales, 0, PASSES, N_TILE * n, N_TILE)

        def zero_planes(t):
            nc.vector.memset(t[:].bitcast(I32), 0)

        nc.gpsimd.memset(scr_in[:], 0.0)
        nc.vector.memset(ones[:], 1.0)
        zero_planes(w_planes[0])
        nc.vector.memset(brow[:].bitcast(I32), 0)
        zero_planes(x_planes[0])
        make_identity(nc, ident[:])

        cos_v = cos.rearrange("(k p) d -> p k d", p=P)
        sin_v = sin.rearrange("(k p) d -> p k d", p=P)
        half = PASSES // 2
        load_codes(x_codes[0], x_words, 0, 2, 0, 2 * CHUNK_TOKENS, 0)
        load_codes(w_codes[0], Wq_words, 0, 2, 0, 2 * N_TILE, 0)
        load_scales(w_planes[0], Wq_scales, 0, PASSES, 0, N_TILE)
        nc.scalar.dma_start(out=tab_sb[:, 0, :, :], in_=cos_v)
        nc.scalar.dma_start(out=tab_sb[:, 1, :, :], in_=sin_v)
        nc.scalar.dma_start(out=brow[0:1, :], in_=bq.rearrange("(o c) -> o c", o=1))
        nc.scalar.activation(out=scr[:], in_=scr_in[:], func=RELU)
        load_scales(x_planes[0], x_scales, 0, PASSES, 0, CHUNK_TOKENS)
        load_codes(x_codes[0], x_words, 2, half, 0, 2 * CHUNK_TOKENS, 0)
        load_codes(w_codes[0], Wq_words, 2, half, 0, 2 * N_TILE, 0)
        load_codes(x_codes[0], x_words, half, PASSES, 0, 2 * CHUNK_TOKENS, 0)
        load_codes(w_codes[0], Wq_words, half, PASSES, 0, 2 * N_TILE, 0)

        def flip_sign(k0, k1):
            even = tab_sb[:, 1, k0:k1, :].rearrange("p k (i e) -> p k i e", e=2)[:, :, :, 0:1]
            nc.scalar.activation(out=even, in_=even, func=COPY, scale=-1.0)

        def table_to_psum(j, t):
            nc.tensor.matmul(
                tab_ps[j][:, 2 * D * t : 2 * D * (t + 1)],
                lhsT=ident[:],
                rhs=tab_sb[:, t, 2 * j : 2 * j + 2, :].rearrange("p k d -> p (k d)"),
                start=True,
                stop=True,
            )

        warm = accs.tile([P, N_TILE], F32, name="acc")
        for r in range(N_WARM):
            nc.tensor.matmul(warm[:, 0:P], lhsT=ones[:], rhs=ones[:], start=True, stop=True)
        for j in range(POS_BLOCKS // 2):
            table_to_psum(j, 0)
        for n in range(N_BLOCKS):
            pb = accs.tile([P, N_TILE], F32, name="acc")
            nc.tensor.matmul(pb[:], lhsT=ones[:], rhs=brow[:, N_TILE * n : N_TILE * (n + 1)], start=True, stop=True)
            nc.vector.tensor_copy(out=bias_sb[:, N_TILE * n : N_TILE * (n + 1)], in_=pb[:])
        for j in range(POS_BLOCKS // 2):
            flip_sign(2 * j, 2 * j + 2)
            table_to_psum(j, 1)

        for n in range(1, N_BLOCKS):
            zero_planes(w_planes[n])
        zero_planes(x_planes[1])
        load_w_block(1)
        load_w_block(2)
        load_w_block(3)
        load_x_chunk(1)

        def pairs(ap):
            return ap.rearrange("p (i e) -> p i e", e=2)

        def passes(acc, c, n, mm, g0, g1):
            xc = x_codes[c % X_BUFS]
            xp = x_planes[c % X_BUFS]
            for g in range(g0, g1):
                nc.tensor.matmul_mx(
                    out=acc[:],
                    lhsT=xc[:, g, 2 * P * mm : 2 * P * (mm + 1)].bitcast(FP4X4),
                    lhsT_scale=xp[:, g, P * mm : P * (mm + 1)],
                    rhs=w_codes[n][:, g, :].bitcast(FP4X4),
                    rhs_scale=w_planes[n][:, g, :],
                    start=(g == 0),
                    stop=(g == PASSES - 1),
                )

        def project(c, n, mm):
            acc = accs.tile([P, N_TILE], F32, name="acc")
            passes(acc, c, n, mm, 0, PASSES)
            return acc

        def epilogue(acc, m, n, last):
            b = m // POS_BLOCKS
            k = m % POS_BLOCKS
            cos_p = tab_ps[k // 2][:, D * (k % 2) : D * (k % 2 + 1)]
            sin_p = tab_ps[k // 2][:, 2 * D + D * (k % 2) : 2 * D + D * (k % 2 + 1)]
            y = work.tile([P, N_TILE], F32, name="y")
            t1 = work.tile([P, N_TILE], F32, name="t1")
            t2 = work.tile([P, N_TILE], F32, name="t2")
            z = work.tile([P, N_TILE], F32, name="z")
            o = work.tile([P, N_TILE], F32, name="o")
            heads = [slice(D * h, D * (h + 1)) for h in range(N_TILE // D)]
            for sl in heads:
                nc.vector.tensor_tensor(out=y[:, sl], in0=acc[:, sl], in1=bias_sb[:, N_TILE * n + sl.start : N_TILE * n + sl.stop], op=ADD)
            for sl in heads:
                nc.vector.tensor_tensor(out=t1[:, sl], in0=y[:, sl], in1=cos_p, op=MULT)
            for sl in heads:
                nc.vector.tensor_tensor(out=pairs(t2[:, sl]), in0=pairs(y[:, sl])[:, :, ::-1], in1=pairs(sin_p), op=MULT)
            adder = nc.vector if last else nc.gpsimd
            for sl in heads if last else [slice(0, N_TILE)]:
                adder.tensor_tensor(out=z[:, sl], in0=t1[:, sl], in1=t2[:, sl], op=ADD)
                final = last and sl.stop == N_TILE
                if final:
                    nc.vector.tensor_scalar_max(out=o[:, sl], in0=z[:, sl], scalar1=0.0)
                else:
                    nc.scalar.activation(out=o[:, sl], in_=z[:, sl], func=RELU)
                h0 = (N_TILE * n + sl.start) // D
                h1 = (N_TILE * n + sl.stop) // D
                queue = nc.sync if final else nc.scalar
                queue.dma_start(
                    out=out[b, h0:h1, P * k : P * (k + 1), :].rearrange("h p d -> p h d"),
                    in_=o[:, sl].rearrange("p (h d) -> p h d", d=D),
                )

        first = []
        for mm in range(CHUNK_BLOCKS):
            first.append(accs.tile([P, N_TILE], F32, name="acc"))
        for g in range(PASSES):
            for mm in range(CHUNK_BLOCKS):
                passes(first[mm], 0, 0, mm, g, g + 1)
        for mm in range(CHUNK_BLOCKS):
            epilogue(first[mm], mm, 0, False)

        for c in range(N_CHUNKS):
            for n in range(N_BLOCKS):
                for mm in range(CHUNK_BLOCKS):
                    if (c, n) != (0, 0):
                        acc = project(c, n, mm)
                        epilogue(acc, CHUNK_BLOCKS * c + mm, n, (c, n, mm) == (N_CHUNKS - 1, N_BLOCKS - 1, CHUNK_BLOCKS - 1))
            if c + X_BUFS < N_CHUNKS:
                load_x_chunk(c + X_BUFS)
